import numpy as np
import ml_dtypes


def mxq(x, axis, fmt="e4m3"):
    dtype, down = {"e4m3": (ml_dtypes.float8_e4m3fn, 7), "e5m2": (ml_dtypes.float8_e5m2, 14)}[fmt]
    v = np.moveaxis(np.asarray(x, np.float32).astype(ml_dtypes.bfloat16).astype(np.float64), axis, -1)
    blocks = v.reshape(v.shape[:-1] + (-1, 32))
    amax = np.abs(blocks).max(-1, keepdims=True)
    byte = np.maximum(np.where(amax > 0, np.frexp(amax)[1] - 1 + 127, 0) - down, 1)
    scale = np.exp2(byte - 127.0)
    codes = (blocks / scale).astype(np.float32).astype(dtype).astype(np.float64)
    return np.moveaxis((codes * scale).reshape(v.shape), -1, axis)


WIDE = False


def mx_kscale(k):
    if not WIDE:
        return np.ones(k)
    levels = np.array([10, -10, 5, -5, 0])
    a = np.random.permutation(np.resize(levels, k // 512 * 4)).reshape(k // 512, 4)
    idx = np.arange(k)
    return np.exp2(a[idx // 512, idx % 128 // 32])


BF16 = ml_dtypes.bfloat16


def bf(x):
    return np.asarray(x, np.float32).astype(BF16)


def f64(x):
    return np.asarray(x).astype(np.float64)


B, NSEG, SEGLEN, HEADS, D, E, I = 1, 4, 256, 2, 512, 16, 512
S = NSEG * SEGLEN
HID = HEADS * D
NPREV = NSEG - 1


def softmax(v):
    e = np.exp(v - v.max(-1, keepdims=True))
    return e / e.sum(-1, keepdims=True)


def merge(w, ew):
    m = 0.0
    for e in range(E):
        m = m + ew[..., e, None, None] * w[e]
    return m


def setup_inputs():
    s, t = mx_kscale(D), mx_kscale(I)
    return {'x_mh': bf(np.random.standard_normal((B, S, HID)) * np.tile(s, HEADS)),
            'ew': bf(softmax(1.5 * np.random.standard_normal((B, NPREV, HEADS, E)))),
            'first_linear': bf(np.random.standard_normal((E, I, D)) * 2.0 / np.sqrt(D) * t[:, None] / s),
            'second_linear': bf(np.random.standard_normal((E, D, I)) * 2.0 / np.sqrt(I) / t)}


def reference(x_mh, ew, first_linear, second_linear):
    w = f64(ew)
    m1q = mxq(merge(f64(first_linear), w), 4, 'e4m3')
    m2q = mxq(merge(f64(second_linear), w), 4, 'e4m3')
    xr = f64(x_mh).reshape(B, NSEG, SEGLEN, HEADS, D).reshape(B, NSEG, HEADS, SEGLEN, D)
    xq = mxq(xr, 4, 'e4m3')
    h = np.maximum(xq[:, 1:] @ m1q.swapaxes(-1, -2), 0.0)
    res = mxq(h, 4, 'e4m3') @ m2q.swapaxes(-1, -2)
    h0 = np.maximum(xq[:, 0] @ m1q[:, 0].swapaxes(-1, -2), 0.0)
    r0 = mxq(h0, 3, 'e4m3') @ m2q[:, 0].swapaxes(-1, -2)
    out = np.concatenate([r0[:, None], res], axis=1)
    return out.reshape(B, S, HEADS, D).reshape(B, S, HID)

@@ -1,0 +1,277 @@
+from contextlib import ExitStack
+
+import concourse.mybir as mybir
+from concourse.masks import make_identity
+
+FP8X4 = mybir.dt.float8_e4m3fn_x4
+BF16 = mybir.dt.bfloat16
+F32 = mybir.dt.float32
+U32 = mybir.dt.uint32
+U8 = mybir.dt.uint8
+ADD = mybir.AluOpType.add
+MULT = mybir.AluOpType.mult
+AXIS_X = mybir.AxisListType.X
+RELU = mybir.ActivationFunctionType.Relu
+COPY = mybir.ActivationFunctionType.Copy
+
+P = 128
+PACK = 4
+EXPERTS = 16
+MIXES = 6
+DIM = 512
+ROWS = 2048
+ROW_TILES = ROWS // P
+WORD_COLS = P * PACK
+
+LANES = P // EXPERTS
+LANE_ROWS = P // LANES
+PAIR = 2
+UNIT_TILES = (1, 2, 3)
+CHAINS = 2
+TERMS = CHAINS + EXPERTS // 2
+LOAD_EXPERTS = 4
+LOAD_AHEAD = 3
+
+FLOPS = 2 * 2 * ROWS * DIM * DIM + 2 * 2 * MIXES * EXPERTS * DIM * DIM
+
+
+def mix_of_row_tile(rt):
+    block = rt // 2
+    segment, group = block // 2, block % 2
+    return max(segment - 1, 0) * 2 + group
+
+
+def tile_mh_lori_pa_kernel(tc, x_mh, ew, first_linear, second_linear, out):
+    nc = tc.nc
+    x_rows = x_mh.rearrange("b s (h d) -> (b s h) d", d=DIM)
+    out_rows = out.rearrange("b s (h d) -> (b s h) d", d=DIM)
+    weights = (first_linear, second_linear)
+    tiles_of_mix = [[rt for rt in range(ROW_TILES) if mix_of_row_tile(rt) == q] for q in range(MIXES)]
+    h_order = [rt for q in range(MIXES) for rt in tiles_of_mix[q]]
+
+    with ExitStack() as ctx:
+        const = ctx.enter_context(tc.tile_pool(name="const", bufs=1))
+        keep = ctx.enter_context(tc.tile_pool(name="keep", bufs=1))
+        wpool = ctx.enter_context(tc.tile_pool(name="wpool", bufs=3))
+        lanes = ctx.enter_context(tc.tile_pool(name="lanes", bufs=1))
+        tpool = ctx.enter_context(tc.tile_pool(name="tpool", bufs=2))
+        stage = ctx.enter_context(tc.tile_pool(name="stage", bufs=4))
+        opool = ctx.enter_context(tc.tile_pool(name="opool", bufs=4))
+        psum_unit = ctx.enter_context(tc.psum_pool(name="psum_unit", bufs=2))
+        psum_lane = ctx.enter_context(tc.psum_pool(name="psum_lane", bufs=2))
+        psum_turn = ctx.enter_context(tc.psum_pool(name="psum_turn", bufs=2))
+        psum_out = ctx.enter_context(tc.psum_pool(name="psum_out", bufs=2))
+
+        def load_rows(n, u):
+            w_rows = wpool.tile([P, EXPERTS, DIM], BF16, name="w_rows")
+            for first in range(0, EXPERTS, LOAD_EXPERTS):
+                some = slice(first, first + LOAD_EXPERTS)
+                nc.sync.dma_start(
+                    out=w_rows[:, some, :],
+                    in_=weights[n][some, u * P : (u + 1) * P, :].rearrange("e p c -> p e c"),
+                )
+            return w_rows
+
+        ew_all = const.tile([P, MIXES, EXPERTS], BF16)
+        nc.sync.dma_start(
+            out=ew_all[:].rearrange("p q e -> p (q e)"),
+            in_=ew.rearrange("b n g e -> (b n g e)").partition_broadcast(P),
+        )
+        units = [(0, q, u) for u in UNIT_TILES for q in range(MIXES)]
+        units += [(1, q, u) for q in range(MIXES) for u in UNIT_TILES]
+        loaded = {(0, UNIT_TILES[0]): load_rows(0, UNIT_TILES[0])}
+
+        ident_bf = const.tile([P, P], BF16)
+        make_identity(nc, ident_bf[:])
+        ident_f32 = const.tile([P, P], F32)
+        make_identity(nc, ident_f32[:])
+        ew_f32 = const.tile([P, MIXES * EXPERTS], F32)
+        nc.vector.tensor_copy(out=ew_f32[:], in_=ew_all[:].rearrange("p q e -> p (q e)"))
+
+        own_expert = const.tile([P, EXPERTS], F32)
+        nc.vector.tensor_reduce(
+            out=own_expert[:], in_=ident_bf[:].rearrange("p (r e) -> p e r", e=EXPERTS), axis=AXIS_X, op=ADD
+        )
+        own_lane = const.tile([P, LANES], F32)
+        nc.vector.tensor_reduce(
+            out=own_lane[:], in_=ident_bf[:].rearrange("p (r e) -> p r e", e=EXPERTS), axis=AXIS_X, op=ADD
+        )
+        picked = const.tile([P, MIXES, EXPERTS], F32)
+        nc.vector.tensor_tensor(
+            out=picked[:],
+            in0=ew_all[:],
+            in1=own_expert[:].unsqueeze(1).to_broadcast([P, MIXES, EXPERTS]),
+            op=MULT,
+        )
+        ew_own = const.tile([P, MIXES], F32)
+        nc.vector.tensor_reduce(out=ew_own[:], in_=picked[:], axis=AXIS_X, op=ADD)
+        ew_diag = const.tile([P, MIXES, LANES], BF16)
+        nc.vector.tensor_tensor(
+            out=ew_diag[:],
+            in0=ew_own[:].unsqueeze(2).to_broadcast([P, MIXES, LANES]),
+            in1=own_lane[:].unsqueeze(1).to_broadcast([P, MIXES, LANES]),
+            op=MULT,
+        )
+
+        grouped = [
+            keep.tile([P, MIXES, DIM * PACK], BF16, align_bytes=64, name="grouped_%d" % n) for n in range(2)
+        ]
+        x_codes = keep.tile([P, ROWS], U32, align_bytes=64)
+        x_scales = keep.tile([P, ROWS], U8, align_bytes=64)
+        h_codes = keep.tile([P, ROWS], U32, align_bytes=64)
+        h_scales = keep.tile([P, ROWS], U8, align_bytes=64)
+        m_codes = [keep.tile([P, MIXES, DIM], U32, align_bytes=64, name="m_codes_%d" % n) for n in range(2)]
+        m_scales = [keep.tile([P, MIXES, DIM], U8, align_bytes=64, name="m_scales_%d" % n) for n in range(2)]
+
+        def quantise_x():
+            tiles = ROW_TILES // 4
+            for part in range(4):
+                x_sb = stage.tile([P, tiles, DIM], BF16, align_bytes=64, tag="stage")
+                nc.sync.dma_start(
+                    out=x_sb[:],
+                    in_=x_rows[part * tiles * P : (part + 1) * tiles * P, :].rearrange("(a p) d -> p a d", p=P),
+                )
+                x_grouped = stage.tile([P, tiles, P, PACK], BF16, align_bytes=64, tag="stage")
+                for a in range(tiles):
+                    x_turned = psum_turn.tile([P, PACK, P], BF16, tag="turn")
+                    for t in range(PACK):
+                        nc.tensor.transpose(x_turned[:, t, :], x_sb[:, a, t * P : (t + 1) * P], ident_bf[:])
+                    nc.scalar.copy(out=x_grouped[:, a, :, :], in_=x_turned[:].rearrange("p t r -> p r t"))
+                cols = slice(part * tiles * P, (part + 1) * tiles * P)
+                nc.vector.quantize_mx(
+                    out=x_codes[:, cols].bitcast(FP8X4),
+                    scales=x_scales[:, cols],
+                    in_=x_grouped[:].rearrange("p a r t -> p (a r t)"),
+                )
+
+        def merge_by_matmul(n):
+            w_lanes = lanes.tile([P, LANE_ROWS, DIM], BF16)
+            for r in range(LANES):
+                nc.sync.dma_start(
+                    out=w_lanes[r * EXPERTS : (r + 1) * EXPERTS, :, :].rearrange("e j c -> e (j c)"),
+                    in_=weights[n][:, r * LANE_ROWS : (r + 1) * LANE_ROWS, :].rearrange("e j c -> e (j c)"),
+                )
+            by_pair = grouped[n][:, :, 0:WORD_COLS].rearrange("p q (r j x) -> p q r j x", r=LANES, x=PAIR * PACK)
+            for pair in range(LANE_ROWS // PAIR):
+                sums = psum_lane.tile([P, MIXES, LANES, PAIR, PACK], F32)
+                for b in range(PAIR):
+                    for t in range(PACK):
+                        nc.tensor.matmul(
+                            out=sums[:, :, :, b, t],
+                            lhsT=w_lanes[:, pair * PAIR + b, t * P : (t + 1) * P],
+                            rhs=ew_diag[:],
+                            start=True,
+                            stop=True,
+                        )
+                nc.vector.tensor_copy(
+                    out=by_pair[:, :, :, pair, :], in_=sums[:].rearrange("p q r b t -> p q r (b t)")
+                )
+
+        def make_terms(w_rows, q):
+            terms = tpool.tile([P, TERMS, DIM], F32)
+            for e in range(EXPERTS):
+                share = ew_f32[:, q * EXPERTS + e : q * EXPERTS + e + 1]
+                if e % 2 == 1:
+                    nc.scalar.activation(
+                        out=terms[:, CHAINS + e // 2, :], in_=w_rows[:, e, :], func=COPY, scale=share
+                    )
+                elif e // 2 < CHAINS:
+                    nc.vector.tensor_scalar_mul(out=terms[:, e // 2, :], in0=w_rows[:, e, :], scalar1=share)
+                else:
+                    chain = terms[:, (e // 2) % CHAINS, :]
+                    nc.vector.scalar_tensor_tensor(
+                        out=chain, in0=w_rows[:, e, :], scalar=share, in1=chain, op0=MULT, op1=ADD
+                    )
+            return terms
+
+        def collect(terms, n, q, u):
+            turned = psum_unit.tile([P, PACK, P], F32)
+            for t in range(PACK):
+                for i in range(TERMS):
+                    term = (i + CHAINS) % TERMS
+                    nc.tensor.matmul(
+                        out=turned[:, t, :],
+                        lhsT=terms[:, term, t * P : (t + 1) * P],
+                        rhs=ident_f32[:],
+                        is_transpose=True,
+                        start=(i == 0),
+                        stop=(i == TERMS - 1),
+                    )
+            nc.vector.tensor_copy(
+                out=grouped[n][:, q, u * WORD_COLS : (u + 1) * WORD_COLS].rearrange("p (r t) -> p r t", t=PACK),
+                in_=turned[:].rearrange("p t r -> p r t"),
+            )
+
+        def hidden_layer(q):
+            mine = tiles_of_mix[q]
+            h_grouped = stage.tile([P, len(mine), P, PACK], BF16, align_bytes=64, tag="stage")
+            for a, rt in enumerate(mine):
+                rows = slice(rt * P, (rt + 1) * P)
+                h_bank = psum_turn.tile([P, PACK, P], F32, tag="turn")
+                for t in range(PACK):
+                    hidden = slice(t * P, (t + 1) * P)
+                    nc.tensor.matmul_mx(
+                        out=h_bank[:, t, :],
+                        lhsT=m_codes[0][:, q, hidden].bitcast(FP8X4),
+                        lhsT_scale=m_scales[0][:, q, hidden],
+                        rhs=x_codes[:, rows].bitcast(FP8X4),
+                        rhs_scale=x_scales[:, rows],
+                        start=True,
+                        stop=True,
+                    )
+                nc.scalar.activation(
+                    out=h_grouped[:, a, :, :], in_=h_bank[:].rearrange("p t r -> p r t"), func=RELU
+                )
+            first = h_order.index(mine[0])
+            cols = slice(first * P, (first + len(mine)) * P)
+            nc.vector.quantize_mx(
+                out=h_codes[:, cols].bitcast(FP8X4),
+                scales=h_scales[:, cols],
+                in_=h_grouped[:].rearrange("p a r t -> p (a r t)"),
+            )
+
+        def output_layer(q):
+            for rt in tiles_of_mix[q]:
+                place = h_order.index(rt)
+                cols = slice(place * P, (place + 1) * P)
+                o_bank = psum_out.tile([P, DIM], F32)
+                nc.tensor.matmul_mx(
+                    out=o_bank[:],
+                    lhsT=h_codes[:, cols].bitcast(FP8X4),
+                    lhsT_scale=h_scales[:, cols],
+                    rhs=m_codes[1][:, q, :].bitcast(FP8X4),
+                    rhs_scale=m_scales[1][:, q, :],
+                    start=True,
+                    stop=True,
+                )
+                o_sb = opool.tile([P, DIM], F32)
+                nc.scalar.copy(out=o_sb[:], in_=o_bank[:])
+                nc.sync.dma_start(out=out_rows[rt * P : (rt + 1) * P, :], in_=o_sb[:])
+
+        terms_before = None
+        for i in range(len(units) + 1):
+            terms_now = None
+            if i < len(units):
+                n, q, u = units[i]
+                terms_now = make_terms(loaded[(n, u)], q)
+                for n, q, u in units[i + 1 : i + 1 + LOAD_AHEAD]:
+                    if (n, u) not in loaded:
+                        loaded[(n, u)] = load_rows(n, u)
+            if i > 0:
+                n, q, u = units[i - 1]
+                collect(terms_before, n, q, u)
+                if u == UNIT_TILES[-1]:
+                    nc.vector.quantize_mx(
+                        out=m_codes[n][:, q, :].bitcast(FP8X4), scales=m_scales[n][:, q, :], in_=grouped[n][:, q, :]
+                    )
+                    if n == 0:
+                        hidden_layer(q)
+                    else:
+                        output_layer(q)
+            terms_before = terms_now
+            if i == 1:
+                quantise_x()
+            if i == 3:
+                merge_by_matmul(0)
+            if i == 5:
+                merge_by_matmul(1)

@@ -28,7 +28,8 @@ LANE_ROWS = P // LANES
 PAIR = 2
 UNIT_TILES = (1, 2, 3)
 CHAINS = 2
-TERMS = CHAINS + EXPERTS // 2
+SCALAR_SHARE = 7
+TERMS = CHAINS + SCALAR_SHARE
 LOAD_EXPERTS = 4
 LOAD_AHEAD = 3
 
@@ -169,19 +170,22 @@ def tile_mh_lori_pa_kernel(tc, x_mh, ew, first_linear, second_linear, out):
 
         def make_terms(w_rows, q):
             terms = tpool.tile([P, TERMS, DIM], F32)
+            turn = 0
             for e in range(EXPERTS):
                 share = ew_f32[:, q * EXPERTS + e : q * EXPERTS + e + 1]
-                if e % 2 == 1:
+                if e % 2 == 1 and e // 2 < SCALAR_SHARE:
                     nc.scalar.activation(
                         out=terms[:, CHAINS + e // 2, :], in_=w_rows[:, e, :], func=COPY, scale=share
                     )
-                elif e // 2 < CHAINS:
-                    nc.vector.tensor_scalar_mul(out=terms[:, e // 2, :], in0=w_rows[:, e, :], scalar1=share)
                 else:
-                    chain = terms[:, (e // 2) % CHAINS, :]
-                    nc.vector.scalar_tensor_tensor(
-                        out=chain, in0=w_rows[:, e, :], scalar=share, in1=chain, op0=MULT, op1=ADD
-                    )
+                    chain = terms[:, turn % CHAINS, :]
+                    if turn < CHAINS:
+                        nc.vector.tensor_scalar_mul(out=chain, in0=w_rows[:, e, :], scalar1=share)
+                    else:
+                        nc.vector.scalar_tensor_tensor(
+                            out=chain, in0=w_rows[:, e, :], scalar=share, in1=chain, op0=MULT, op1=ADD
+                        )
+                    turn += 1
             return terms
 
         def collect(terms, n, q, u):

from contextlib import ExitStack

import concourse.mybir as mybir
from concourse.masks import make_identity

FP8X4 = mybir.dt.float8_e4m3fn_x4
BF16 = mybir.dt.bfloat16
F32 = mybir.dt.float32
U32 = mybir.dt.uint32
U8 = mybir.dt.uint8
ADD = mybir.AluOpType.add
MULT = mybir.AluOpType.mult
AXIS_X = mybir.AxisListType.X
RELU = mybir.ActivationFunctionType.Relu
COPY = mybir.ActivationFunctionType.Copy

P = 128
PACK = 4
EXPERTS = 16
MIXES = 6
DIM = 512
ROWS = 2048
ROW_TILES = ROWS // P
WORD_COLS = P * PACK

LANES = P // EXPERTS
LANE_ROWS = P // LANES
PAIR = 2
UNIT_TILES = (1, 2, 3)
CHAINS = 2
SCALAR_SHARE = 7
TERMS = CHAINS + SCALAR_SHARE
LOAD_EXPERTS = 4
LOAD_AHEAD = 3

FLOPS = 2 * 2 * ROWS * DIM * DIM + 2 * 2 * MIXES * EXPERTS * DIM * DIM


def mix_of_row_tile(rt):
    block = rt // 2
    segment, group = block // 2, block % 2
    return max(segment - 1, 0) * 2 + group


def tile_mh_lori_pa_kernel(tc, x_mh, ew, first_linear, second_linear, out):
    nc = tc.nc
    x_rows = x_mh.rearrange("b s (h d) -> (b s h) d", d=DIM)
    out_rows = out.rearrange("b s (h d) -> (b s h) d", d=DIM)
    weights = (first_linear, second_linear)
    tiles_of_mix = [[rt for rt in range(ROW_TILES) if mix_of_row_tile(rt) == q] for q in range(MIXES)]
    h_order = [rt for q in range(MIXES) for rt in tiles_of_mix[q]]

    with ExitStack() as ctx:
        const = ctx.enter_context(tc.tile_pool(name="const", bufs=1))
        keep = ctx.enter_context(tc.tile_pool(name="keep", bufs=1))
        wpool = ctx.enter_context(tc.tile_pool(name="wpool", bufs=3))
        lanes = ctx.enter_context(tc.tile_pool(name="lanes", bufs=1))
        tpool = ctx.enter_context(tc.tile_pool(name="tpool", bufs=2))
        stage = ctx.enter_context(tc.tile_pool(name="stage", bufs=4))
        opool = ctx.enter_context(tc.tile_pool(name="opool", bufs=4))
        psum_unit = ctx.enter_context(tc.psum_pool(name="psum_unit", bufs=2))
        psum_lane = ctx.enter_context(tc.psum_pool(name="psum_lane", bufs=2))
        psum_turn = ctx.enter_context(tc.psum_pool(name="psum_turn", bufs=2))
        psum_out = ctx.enter_context(tc.psum_pool(name="psum_out", bufs=2))

        def load_rows(n, u):
            w_rows = wpool.tile([P, EXPERTS, DIM], BF16, name="w_rows")
            for first in range(0, EXPERTS, LOAD_EXPERTS):
                some = slice(first, first + LOAD_EXPERTS)
                nc.sync.dma_start(
                    out=w_rows[:, some, :],
                    in_=weights[n][some, u * P : (u + 1) * P, :].rearrange("e p c -> p e c"),
                )
            return w_rows

        ew_all = const.tile([P, MIXES, EXPERTS], BF16)
        nc.sync.dma_start(
            out=ew_all[:].rearrange("p q e -> p (q e)"),
            in_=ew.rearrange("b n g e -> (b n g e)").partition_broadcast(P),
        )
        units = [(0, q, u) for u in UNIT_TILES for q in range(MIXES)]
        units += [(1, q, u) for q in range(MIXES) for u in UNIT_TILES]
        loaded = {(0, UNIT_TILES[0]): load_rows(0, UNIT_TILES[0])}

        ident_bf = const.tile([P, P], BF16)
        make_identity(nc, ident_bf[:])
        ident_f32 = const.tile([P, P], F32)
        make_identity(nc, ident_f32[:])
        ew_f32 = const.tile([P, MIXES * EXPERTS], F32)
        nc.vector.tensor_copy(out=ew_f32[:], in_=ew_all[:].rearrange("p q e -> p (q e)"))

        own_expert = const.tile([P, EXPERTS], F32)
        nc.vector.tensor_reduce(
            out=own_expert[:], in_=ident_bf[:].rearrange("p (r e) -> p e r", e=EXPERTS), axis=AXIS_X, op=ADD
        )
        own_lane = const.tile([P, LANES], F32)
        nc.vector.tensor_reduce(
            out=own_lane[:], in_=ident_bf[:].rearrange("p (r e) -> p r e", e=EXPERTS), axis=AXIS_X, op=ADD
        )
        picked = const.tile([P, MIXES, EXPERTS], F32)
        nc.vector.tensor_tensor(
            out=picked[:],
            in0=ew_all[:],
            in1=own_expert[:].unsqueeze(1).to_broadcast([P, MIXES, EXPERTS]),
            op=MULT,
        )
        ew_own = const.tile([P, MIXES], F32)
        nc.vector.tensor_reduce(out=ew_own[:], in_=picked[:], axis=AXIS_X, op=ADD)
        ew_diag = const.tile([P, MIXES, LANES], BF16)
        nc.vector.tensor_tensor(
            out=ew_diag[:],
            in0=ew_own[:].unsqueeze(2).to_broadcast([P, MIXES, LANES]),
            in1=own_lane[:].unsqueeze(1).to_broadcast([P, MIXES, LANES]),
            op=MULT,
        )

        grouped = [
            keep.tile([P, MIXES, DIM * PACK], BF16, align_bytes=64, name="grouped_%d" % n) for n in range(2)
        ]
        x_codes = keep.tile([P, ROWS], U32, align_bytes=64)
        x_scales = keep.tile([P, ROWS], U8, align_bytes=64)
        h_codes = keep.tile([P, ROWS], U32, align_bytes=64)
        h_scales = keep.tile([P, ROWS], U8, align_bytes=64)
        m_codes = [keep.tile([P, MIXES, DIM], U32, align_bytes=64, name="m_codes_%d" % n) for n in range(2)]
        m_scales = [keep.tile([P, MIXES, DIM], U8, align_bytes=64, name="m_scales_%d" % n) for n in range(2)]

        def quantise_x():
            tiles = ROW_TILES // 4
            for part in range(4):
                x_sb = stage.tile([P, tiles, DIM], BF16, align_bytes=64, tag="stage")
                nc.sync.dma_start(
                    out=x_sb[:],
                    in_=x_rows[part * tiles * P : (part + 1) * tiles * P, :].rearrange("(a p) d -> p a d", p=P),
                )
                x_grouped = stage.tile([P, tiles, P, PACK], BF16, align_bytes=64, tag="stage")
                for a in range(tiles):
                    x_turned = psum_turn.tile([P, PACK, P], BF16, tag="turn")
                    for t in range(PACK):
                        nc.tensor.transpose(x_turned[:, t, :], x_sb[:, a, t * P : (t + 1) * P], ident_bf[:])
                    nc.scalar.copy(out=x_grouped[:, a, :, :], in_=x_turned[:].rearrange("p t r -> p r t"))
                cols = slice(part * tiles * P, (part + 1) * tiles * P)
                nc.vector.quantize_mx(
                    out=x_codes[:, cols].bitcast(FP8X4),
                    scales=x_scales[:, cols],
                    in_=x_grouped[:].rearrange("p a r t -> p (a r t)"),
                )

        def merge_by_matmul(n):
            w_lanes = lanes.tile([P, LANE_ROWS, DIM], BF16)
            for r in range(LANES):
                nc.sync.dma_start(
                    out=w_lanes[r * EXPERTS : (r + 1) * EXPERTS, :, :].rearrange("e j c -> e (j c)"),
                    in_=weights[n][:, r * LANE_ROWS : (r + 1) * LANE_ROWS, :].rearrange("e j c -> e (j c)"),
                )
            by_pair = grouped[n][:, :, 0:WORD_COLS].rearrange("p q (r j x) -> p q r j x", r=LANES, x=PAIR * PACK)
            for pair in range(LANE_ROWS // PAIR):
                sums = psum_lane.tile([P, MIXES, LANES, PAIR, PACK], F32)
                for b in range(PAIR):
                    for t in range(PACK):
                        nc.tensor.matmul(
                            out=sums[:, :, :, b, t],
                            lhsT=w_lanes[:, pair * PAIR + b, t * P : (t + 1) * P],
                            rhs=ew_diag[:],
                            start=True,
                            stop=True,
                        )
                nc.vector.tensor_copy(
                    out=by_pair[:, :, :, pair, :], in_=sums[:].rearrange("p q r b t -> p q r (b t)")
                )

        def make_terms(w_rows, q):
            terms = tpool.tile([P, TERMS, DIM], F32)
            turn = 0
            for e in range(EXPERTS):
                share = ew_f32[:, q * EXPERTS + e : q * EXPERTS + e + 1]
                if e % 2 == 1 and e // 2 < SCALAR_SHARE:
                    nc.scalar.activation(
                        out=terms[:, CHAINS + e // 2, :], in_=w_rows[:, e, :], func=COPY, scale=share
                    )
                else:
                    chain = terms[:, turn % CHAINS, :]
                    if turn < CHAINS:
                        nc.vector.tensor_scalar_mul(out=chain, in0=w_rows[:, e, :], scalar1=share)
                    else:
                        nc.vector.scalar_tensor_tensor(
                            out=chain, in0=w_rows[:, e, :], scalar=share, in1=chain, op0=MULT, op1=ADD
                        )
                    turn += 1
            return terms

        def collect(terms, n, q, u):
            turned = psum_unit.tile([P, PACK, P], F32)
            for t in range(PACK):
                for i in range(TERMS):
                    term = (i + CHAINS) % TERMS
                    nc.tensor.matmul(
                        out=turned[:, t, :],
                        lhsT=terms[:, term, t * P : (t + 1) * P],
                        rhs=ident_f32[:],
                        is_transpose=True,
                        start=(i == 0),
                        stop=(i == TERMS - 1),
                    )
            nc.vector.tensor_copy(
                out=grouped[n][:, q, u * WORD_COLS : (u + 1) * WORD_COLS].rearrange("p (r t) -> p r t", t=PACK),
                in_=turned[:].rearrange("p t r -> p r t"),
            )

        def hidden_layer(q):
            mine = tiles_of_mix[q]
            h_grouped = stage.tile([P, len(mine), P, PACK], BF16, align_bytes=64, tag="stage")
            for a, rt in enumerate(mine):
                rows = slice(rt * P, (rt + 1) * P)
                h_bank = psum_turn.tile([P, PACK, P], F32, tag="turn")
                for t in range(PACK):
                    hidden = slice(t * P, (t + 1) * P)
                    nc.tensor.matmul_mx(
                        out=h_bank[:, t, :],
                        lhsT=m_codes[0][:, q, hidden].bitcast(FP8X4),
                        lhsT_scale=m_scales[0][:, q, hidden],
                        rhs=x_codes[:, rows].bitcast(FP8X4),
                        rhs_scale=x_scales[:, rows],
                        start=True,
                        stop=True,
                    )
                nc.scalar.activation(
                    out=h_grouped[:, a, :, :], in_=h_bank[:].rearrange("p t r -> p r t"), func=RELU
                )
            first = h_order.index(mine[0])
            cols = slice(first * P, (first + len(mine)) * P)
            nc.vector.quantize_mx(
                out=h_codes[:, cols].bitcast(FP8X4),
                scales=h_scales[:, cols],
                in_=h_grouped[:].rearrange("p a r t -> p (a r t)"),
            )

        def output_layer(q):
            for rt in tiles_of_mix[q]:
                place = h_order.index(rt)
                cols = slice(place * P, (place + 1) * P)
                o_bank = psum_out.tile([P, DIM], F32)
                nc.tensor.matmul_mx(
                    out=o_bank[:],
                    lhsT=h_codes[:, cols].bitcast(FP8X4),
                    lhsT_scale=h_scales[:, cols],
                    rhs=m_codes[1][:, q, :].bitcast(FP8X4),
                    rhs_scale=m_scales[1][:, q, :],
                    start=True,
                    stop=True,
                )
                o_sb = opool.tile([P, DIM], F32)
                nc.scalar.copy(out=o_sb[:], in_=o_bank[:])
                nc.sync.dma_start(out=out_rows[rt * P : (rt + 1) * P, :], in_=o_sb[:])

        terms_before = None
        for i in range(len(units) + 1):
            terms_now = None
            if i < len(units):
                n, q, u = units[i]
                terms_now = make_terms(loaded[(n, u)], q)
                for n, q, u in units[i + 1 : i + 1 + LOAD_AHEAD]:
                    if (n, u) not in loaded:
                        loaded[(n, u)] = load_rows(n, u)
            if i > 0:
                n, q, u = units[i - 1]
                collect(terms_before, n, q, u)
                if u == UNIT_TILES[-1]:
                    nc.vector.quantize_mx(
                        out=m_codes[n][:, q, :].bitcast(FP8X4), scales=m_scales[n][:, q, :], in_=grouped[n][:, q, :]
                    )
                    if n == 0:
                        hidden_layer(q)
                    else:
                        output_layer(q)
            terms_before = terms_now
            if i == 1:
                quantise_x()
            if i == 3:
                merge_by_matmul(0)
            if i == 5:
                merge_by_matmul(1)
